import numpy as np
import ml_dtypes


def mxq(x, axis, fmt="e4m3"):
    dtype, down = {"e4m3": (ml_dtypes.float8_e4m3fn, 7), "e5m2": (ml_dtypes.float8_e5m2, 14)}[fmt]
    v = np.moveaxis(np.asarray(x, np.float32).astype(ml_dtypes.bfloat16).astype(np.float64), axis, -1)
    blocks = v.reshape(v.shape[:-1] + (-1, 32))
    amax = np.abs(blocks).max(-1, keepdims=True)
    byte = np.maximum(np.where(amax > 0, np.frexp(amax)[1] - 1 + 127, 0) - down, 1)
    scale = np.exp2(byte - 127.0)
    codes = (blocks / scale).astype(np.float32).astype(dtype).astype(np.float64)
    return np.moveaxis((codes * scale).reshape(v.shape), -1, axis)


WIDE = False


def mx_kscale(k):
    if not WIDE:
        return np.ones(k)
    levels = np.array([10, -10, 5, -5, 0])
    a = np.random.permutation(np.resize(levels, k // 512 * 4)).reshape(k // 512, 4)
    idx = np.arange(k)
    return np.exp2(a[idx // 512, idx % 128 // 32])


BF16 = ml_dtypes.bfloat16


def bf(x):
    return np.asarray(x, np.float32).astype(BF16)


def f64(x):
    return np.asarray(x).astype(np.float64)


E2M1 = np.array([0.0, 0.5, 1.0, 1.5, 2.0, 3.0, 4.0, 6.0, -0.0, -0.5, -1.0, -1.5, -2.0, -3.0, -4.0, -6.0])


def pack_weight(w, fmt):
    k, n = w.shape
    w = f64(bf(w)).reshape(k // 32, 32, n)
    amax = np.abs(w).max(1)
    if fmt == "e4m3":
        byte = np.frexp(amax)[1] - 1 + 127 - 7
    else:
        mant, ex = np.frexp(amax / 6.0)
        byte = np.where(mant > 0.5, ex, ex - 1) + 127
    byte = np.clip(np.where(amax > 0, byte, 1), 1, 254)
    scaled = (w * np.exp2(127.0 - byte)[:, None, :]).reshape(k, n).astype(np.float32)
    by_word = np.ascontiguousarray(scaled.reshape(k // 512, 128, 4, n).transpose(0, 1, 3, 2))
    if fmt == "e4m3":
        words = by_word.astype(ml_dtypes.float8_e4m3fn).view(np.uint8)
    else:
        c = by_word.astype(ml_dtypes.float4_e2m1fn).view(np.uint8) & 0xF
        words = c[..., 0::2] | (c[..., 1::2] << 4)
    return np.ascontiguousarray(words), np.ascontiguousarray(byte.astype(np.uint8).reshape(k // 512, 16, n))


def unpack_weight(words, scales, fmt):
    g, p, n, _ = words.shape
    if fmt == "e4m3":
        vals = np.ascontiguousarray(words).view(ml_dtypes.float8_e4m3fn).astype(np.float64)
    else:
        nib = np.empty((g, p, n, 4), np.uint8)
        nib[..., 0::2] = words & 0xF
        nib[..., 1::2] = words >> 4
        vals = E2M1[nib]
    vals = vals * np.repeat(np.exp2(scales.astype(np.float64) - 127.0), 8, axis=1)[..., None]
    return vals.transpose(0, 1, 3, 2).reshape(g * 512, n)

def pack4(w):
    words, scales = pack_weight(w, "e2m1")
    return words.reshape(words.shape[0], 128, -1), scales


def unpack4(words, scales):
    return unpack_weight(words.reshape(words.shape[0], 128, -1, 2), scales, "e2m1")


B, S, A, O, H, L = 1024, 1024, 128, 1920, 1024, 384
G = L + A


def sigmoid(v):
    return 1.0 / (1.0 + np.exp(-v))


def setup_inputs():
    s = mx_kscale(G)
    sample = bf(np.random.standard_normal((B, L)) * 1.1 * s[:L])
    prev_action = bf(np.random.standard_normal((B, A)) * s[L:])
    prev_state = bf(np.random.standard_normal((B, S)))
    wih = np.random.standard_normal((3 * H, G)) / np.sqrt(G) / s
    whh = np.random.standard_normal((3 * H, H)) / np.sqrt(H)
    gru_bih = bf(np.random.standard_normal(3 * H) * 0.1)
    gru_bhh = bf(np.random.standard_normal(3 * H) * 0.1)
    wih_words, wih_scales = pack4(np.ascontiguousarray(wih.T))
    whh_words, whh_scales = pack4(np.ascontiguousarray(whh.T))
    return {"sample": sample,
            "prev_action": prev_action,
            "prev_state": prev_state,
            "gru_Wih_words": wih_words,
            "gru_Wih_scales": wih_scales,
            "gru_Whh_words": whh_words,
            "gru_Whh_scales": whh_scales,
            "gru_bih": gru_bih,
            "gru_bhh": gru_bhh}


def reference(sample, prev_action, prev_state, gru_Wih_words, gru_Wih_scales, gru_Whh_words, gru_Whh_scales, gru_bih, gru_bhh):
    hp = f64(prev_state)
    xg = np.concatenate([f64(sample), f64(prev_action)], axis=-1)
    gi = (mxq(xg, 1, "e4m3") @ unpack4(gru_Wih_words, gru_Wih_scales)) + f64(gru_bih)
    gh = (mxq(hp, 1, "e4m3") @ unpack4(gru_Whh_words, gru_Whh_scales)) + f64(gru_bhh)
    gi_r, gi_z, gi_n = np.split(gi, 3, axis=-1)
    gh_r, gh_z, gh_n = np.split(gh, 3, axis=-1)
    r = sigmoid(gi_r + gh_r)
    z = sigmoid(gi_z + gh_z)
    n = np.tanh(gi_n + r * gh_n)
    belief = (1.0 - z) * n + z * hp
    return belief

@@ -1,0 +1,269 @@
+from contextlib import ExitStack
+
+import concourse.mybir as mybir
+from concourse.masks import make_identity
+
+F32 = mybir.dt.float32
+BF16 = mybir.dt.bfloat16
+I32 = mybir.dt.int32
+U32 = mybir.dt.uint32
+U8 = mybir.dt.uint8
+FP8X4 = mybir.dt.float8_e4m3fn_x4
+FP4X4 = mybir.dt.float4_e2m1fn_x4
+ACT = mybir.ActivationFunctionType
+ALU = mybir.AluOpType
+
+P = 128
+BATCH = 1024
+HIDDEN = 1024
+LATENT = 384
+XG = 512
+K_PASS = 512
+PASSES = (XG + HIDDEN) // K_PASS
+WORDS = K_PASS // 2
+TILES = BATCH // P
+PAIRS = TILES // 2
+BANK = 512
+HALVES = BATCH // BANK
+TILES_PER_HALF = BANK // P
+UNITS = HIDDEN // P
+GATE_R, GATE_Z, GATE_N = 0, 1, 2
+
+FLOPS = 2 * BATCH * 3 * HIDDEN * (XG + HIDDEN)
+
+
+def tile_rssm_pb_kernel(
+    tc,
+    sample,
+    prev_action,
+    prev_state,
+    gru_Wih_words,
+    gru_Wih_scales,
+    gru_Whh_words,
+    gru_Whh_scales,
+    gru_bih,
+    gru_bhh,
+    out,
+):
+    nc = tc.nc
+    with ExitStack() as ctx:
+        ctx.enter_context(tc.manual_schedule())
+        resident = ctx.enter_context(tc.tile_pool(name="resident", bufs=1))
+        work = ctx.enter_context(tc.tile_pool(name="work", bufs=4))
+
+        x_rows = resident.tile([P, TILES, XG + HIDDEN], BF16)
+        x_words = x_rows[:].bitcast(F32)
+        x_codes = resident.tile([P, PASSES, BATCH], U32, align_bytes=64)
+        x_scales = resident.tile([P, PASSES, BATCH], U8, align_bytes=64)
+        w_codes = resident.tile([P, PASSES, 2 * 3 * HIDDEN], U8, align_bytes=64)
+        w_scales = resident.tile([P, PASSES, 3 * HIDDEN], U8, align_bytes=64)
+        z_pre = resident.tile([P, TILES, HIDDEN], F32)
+        carried = resident.tile([P, TILES, HIDDEN], F32)
+        identity = resident.tile([P, P], F32)
+        bias_rows = resident.tile([P, HIDDEN], BF16)
+        bias_rows_f32 = resident.tile([P, HIDDEN], F32)
+        z_rows_only = resident.tile([P, P], BF16)
+        bias_z = resident.tile([P, HIDDEN], F32)
+        bias_cols = resident.tile([P, UNITS, P], F32)
+        bias_r = resident.tile([P, UNITS, 1], F32)
+
+        nc.vector.memset(bias_rows[:], 0.0)
+        nc.vector.memset(w_scales[:].bitcast(I32), 0)
+        nc.vector.memset(z_rows_only[:], 0.0)
+        nc.vector.memset(z_rows_only[32:64, :], 1.0)
+        make_identity(nc, identity[:])
+
+        nc.scalar.dma_start(out=bias_rows[0:96:32, :], in_=gru_bih.rearrange("(g n) -> g n", g=3))
+        nc.scalar.dma_start(out=bias_rows[1:97:32, :], in_=gru_bhh.rearrange("(g n) -> g n", g=3))
+
+        sample_rows = sample.rearrange("(p i) c -> p i c", i=TILES)
+        action_rows = prev_action.rearrange("(p i) c -> p i c", i=TILES)
+        state_rows = prev_state.rearrange("(p i) c -> p i c", i=TILES)
+        out_rows = out.rearrange("(p i) h -> p i h", i=TILES)
+
+        def load_pair(pair):
+            tiles = slice(2 * pair, 2 * pair + 2)
+            nc.sync.dma_start(out=x_rows[:, tiles, XG:], in_=state_rows[:, tiles, :])
+            nc.sync.dma_start(out=x_rows[:, tiles, 0:LATENT], in_=sample_rows[:, tiles, :])
+            nc.sync.dma_start(out=x_rows[:, tiles, LATENT:XG], in_=action_rows[:, tiles, :])
+
+        def load_gate_codes(gate):
+            cols = slice(2 * HIDDEN * gate, 2 * HIDDEN * (gate + 1))
+            nc.sync.dma_start(out=w_codes[:, 0, cols].bitcast(I32), in_=gru_Wih_words[0, :, cols].bitcast(I32))
+            nc.sync.dma_start(
+                out=w_codes[:, 1:PASSES, cols].bitcast(I32),
+                in_=gru_Whh_words[:, :, cols].rearrange("g p c -> p g c").bitcast(I32),
+            )
+
+        def load_scales():
+            for s in range(4):
+                nc.sync.dma_start(
+                    out=w_scales[s:P:32, 0, :].bitcast(I32), in_=gru_Wih_scales[0, s:16:4, :].bitcast(I32)
+                )
+                nc.sync.dma_start(
+                    out=w_scales[s:P:32, 1:PASSES, :].bitcast(I32),
+                    in_=gru_Whh_scales[:, s:16:4, :].rearrange("g q n -> q g n").bitcast(I32),
+                )
+
+        load_pair(0)
+        load_gate_codes(GATE_Z)
+        load_scales()
+        for pair in range(1, PAIRS):
+            load_pair(pair)
+        load_gate_codes(GATE_R)
+        load_gate_codes(GATE_N)
+
+        with tc.psum_pool(name="psum_update", bufs=4, reuse_waits="tile") as psum:
+
+            def quantise_pair(pair):
+                grouped_tiles = []
+                for g in range(PASSES):
+                    flipped = psum.tile([P, 2, 2, P], F32, tag="flipped")
+                    for h in range(2):
+                        for u in range(2):
+                            nc.tensor.transpose(
+                                flipped[:, h, u, :],
+                                x_words[:, 2 * pair + h, WORDS * g + u : WORDS * (g + 1) : 2],
+                                identity[:],
+                            )
+                    grouped = work.tile([P, 2 * K_PASS], BF16, align_bytes=64)
+                    grouped_words = grouped[:].bitcast(F32).rearrange("p (h b u) -> p h b u", h=2, u=2)
+                    if (PASSES * pair + g) % 2 == 0:
+                        nc.vector.tensor_copy(out=grouped_words, in_=flipped[:].rearrange("p h u b -> p h b u"))
+                    else:
+                        nc.scalar.copy(out=grouped_words, in_=flipped[:].rearrange("p h u b -> p h b u"))
+                    grouped_tiles.append(grouped)
+                cols = slice(2 * P * pair, 2 * P * (pair + 1))
+                for g in range(PASSES):
+                    nc.vector.quantize_mx(
+                        out=x_codes[:, g, cols].bitcast(FP8X4), scales=x_scales[:, g, cols], in_=grouped_tiles[g][:]
+                    )
+
+            def spread_biases():
+                for half in range(HALVES):
+                    cols = slice(BANK * half, BANK * (half + 1))
+                    repeated = psum.tile([P, BANK], F32, tag="update")
+                    nc.tensor.matmul(repeated[:], lhsT=z_rows_only[:], rhs=bias_rows[:, cols], start=True, stop=True)
+                    nc.scalar.copy(out=bias_z[:, cols], in_=repeated[:])
+                nc.vector.tensor_copy(out=bias_rows_f32[:], in_=bias_rows[:])
+                for half in range(HALVES):
+                    units = slice(TILES_PER_HALF * half, TILES_PER_HALF * (half + 1))
+                    turned = psum.tile([P, TILES_PER_HALF, P], F32, tag="flipped")
+                    for c in range(TILES_PER_HALF):
+                        j = TILES_PER_HALF * half + c
+                        nc.tensor.transpose(turned[:, c, :], bias_rows_f32[:, P * j : P * (j + 1)], identity[:])
+                    nc.scalar.copy(out=bias_cols[:, units, :], in_=turned[:])
+                nc.vector.tensor_tensor(out=bias_r[:], in0=bias_cols[:, :, 0:1], in1=bias_cols[:, :, 1:2], op=ALU.add)
+
+            def update_gate(i):
+                rows = slice(P * i, P * (i + 1))
+                for half in range(HALVES):
+                    cols = slice(BANK * half, BANK * (half + 1))
+                    first = GATE_Z * HIDDEN + BANK * half
+                    update = psum.tile([P, BANK], F32, tag="update")
+                    for g in range(PASSES):
+                        nc.tensor.matmul_mx(
+                            out=update[:],
+                            lhsT=x_codes[:, g, rows].bitcast(FP8X4),
+                            lhsT_scale=x_scales[:, g, rows],
+                            rhs=w_codes[:, g, 2 * first : 2 * (first + BANK)].bitcast(FP4X4),
+                            rhs_scale=w_scales[:, g, first : first + BANK],
+                            start=(g == 0),
+                            stop=(g == PASSES - 1),
+                        )
+                    nc.vector.tensor_tensor(out=z_pre[:, i, cols], in0=update[:], in1=bias_z[:, cols], op=ALU.add)
+                    nc.scalar.activation(out=carried[:, i, cols], in_=z_pre[:, i, cols], func=ACT.Sigmoid)
+                    nc.gpsimd.tensor_tensor(
+                        out=carried[:, i, cols],
+                        in0=carried[:, i, cols],
+                        in1=x_rows[:, i, XG + BANK * half : XG + BANK * (half + 1)],
+                        op=ALU.mult,
+                    )
+
+            quantise_pair(0)
+            spread_biases()
+            for pair in range(PAIRS):
+                update_gate(2 * pair)
+                if pair + 1 < PAIRS:
+                    quantise_pair(pair + 1)
+                update_gate(2 * pair + 1)
+
+        with tc.psum_pool(name="psum_candidate", bufs=2, reuse_waits="tile") as psum:
+
+            def weights_stationary(acc, gate, j, g, half, start, stop):
+                first = gate * HIDDEN + P * j
+                cols = slice(BANK * half, BANK * (half + 1))
+                nc.tensor.matmul_mx(
+                    out=acc[:],
+                    lhsT=w_codes[:, g, 2 * first : 2 * (first + P)].bitcast(FP4X4),
+                    lhsT_scale=w_scales[:, g, first : first + P],
+                    rhs=x_codes[:, g, cols].bitcast(FP8X4),
+                    rhs_scale=x_scales[:, g, cols],
+                    start=start,
+                    stop=stop,
+                )
+
+            def candidate(j):
+                reset_sums, state_sums, input_sums = [], [], []
+                for half in range(HALVES):
+                    reset_sum = psum.tile([P, BANK], F32)
+                    for g in range(PASSES):
+                        weights_stationary(reset_sum, GATE_R, j, g, half, start=(g == 0), stop=(g == PASSES - 1))
+                    reset_sums.append(reset_sum)
+                for half in range(HALVES):
+                    state_sum = psum.tile([P, BANK], F32)
+                    for g in range(1, PASSES):
+                        weights_stationary(state_sum, GATE_N, j, g, half, start=(g == 1), stop=(g == PASSES - 1))
+                    state_sums.append(state_sum)
+                    input_sum = psum.tile([P, BANK], F32)
+                    weights_stationary(input_sum, GATE_N, j, 0, half, start=True, stop=True)
+                    input_sums.append(input_sum)
+
+                inner = []
+                for half in range(HALVES):
+                    reset = work.tile([P, BANK], F32)
+                    nc.scalar.activation(out=reset[:], in_=reset_sums[half][:], func=ACT.Sigmoid, bias=bias_r[:, j, :])
+                    gated = work.tile([P, BANK], F32)
+                    nc.vector.scalar_tensor_tensor(
+                        out=gated[:],
+                        in0=state_sums[half][:],
+                        scalar=bias_cols[:, j, 65:66],
+                        in1=reset[:],
+                        op0=ALU.add,
+                        op1=ALU.mult,
+                    )
+                    inner.append(gated)
+                for half in range(HALVES):
+                    nc.vector.tensor_tensor(out=inner[half][:], in0=inner[half][:], in1=input_sums[half][:], op=ALU.add)
+
+                fresh = work.tile([P, TILES, P], F32)
+                nc.scalar.activation(out=fresh[:], in_=z_pre[:, :, P * j : P * (j + 1)], func=ACT.Sigmoid, scale=-1.0)
+
+                news = []
+                for half in range(HALVES):
+                    new = work.tile([P, BANK], F32)
+                    nc.scalar.activation(out=new[:], in_=inner[half][:], func=ACT.Tanh, bias=bias_cols[:, j, 64:65])
+                    news.append(new)
+                return news, fresh
+
+            def blend_and_store(j, news, fresh):
+                cols = slice(P * j, P * (j + 1))
+                new_rows = []
+                for half in range(HALVES):
+                    turned = psum.tile([P, TILES_PER_HALF, P], F32)
+                    for c in range(TILES_PER_HALF):
+                        nc.tensor.transpose(turned[:, c, :], news[half][:, P * c : P * (c + 1)], identity[:])
+                    new_rows.append(turned)
+                for half in range(HALVES):
+                    tiles = slice(TILES_PER_HALF * half, TILES_PER_HALF * (half + 1))
+                    belief = work.tile([P, TILES_PER_HALF, P], F32)
+                    nc.vector.tensor_tensor(out=belief[:], in0=new_rows[half][:], in1=fresh[:, tiles, :], op=ALU.mult)
+                    nc.gpsimd.tensor_tensor(out=belief[:], in0=belief[:], in1=carried[:, tiles, cols], op=ALU.add)
+                    nc.sync.dma_start(out=out_rows[:, tiles, cols], in_=belief[:])
+
+            waiting = candidate(0)
+            for j in range(1, UNITS):
+                following = candidate(j)
+                blend_and_store(j - 1, waiting[0], waiting[1])
+                waiting = following
+            blend_and_store(UNITS - 1, waiting[0], waiting[1])

@@ -55,7 +55,9 @@ def tile_rssm_pb_kernel(
         x_words = x_rows[:].bitcast(F32)
         x_codes = resident.tile([P, PASSES, BATCH], U32, align_bytes=64)
         x_scales = resident.tile([P, PASSES, BATCH], U8, align_bytes=64)
-        w_codes = resident.tile([P, PASSES, 2 * 3 * HIDDEN], U8, align_bytes=64)
+        w_codes = [
+            resident.tile([P, PASSES, 2 * HIDDEN], U8, align_bytes=64, name="w_codes_%d" % gate) for gate in range(3)
+        ]
         w_scales = resident.tile([P, PASSES, 3 * HIDDEN], U8, align_bytes=64)
         z_pre = resident.tile([P, TILES, HIDDEN], F32)
         carried = resident.tile([P, TILES, HIDDEN], F32)
@@ -75,6 +77,7 @@ def tile_rssm_pb_kernel(
 
         nc.scalar.dma_start(out=bias_rows[0:96:32, :], in_=gru_bih.rearrange("(g n) -> g n", g=3))
         nc.scalar.dma_start(out=bias_rows[1:97:32, :], in_=gru_bhh.rearrange("(g n) -> g n", g=3))
+        nc.vector.tensor_copy(out=bias_rows_f32[:], in_=bias_rows[:])
 
         sample_rows = sample.rearrange("(p i) c -> p i c", i=TILES)
         action_rows = prev_action.rearrange("(p i) c -> p i c", i=TILES)
@@ -89,9 +92,9 @@ def tile_rssm_pb_kernel(
 
         def load_gate_codes(gate):
             cols = slice(2 * HIDDEN * gate, 2 * HIDDEN * (gate + 1))
-            nc.sync.dma_start(out=w_codes[:, 0, cols].bitcast(I32), in_=gru_Wih_words[0, :, cols].bitcast(I32))
+            nc.sync.dma_start(out=w_codes[gate][:, 0, :].bitcast(I32), in_=gru_Wih_words[0, :, cols].bitcast(I32))
             nc.sync.dma_start(
-                out=w_codes[:, 1:PASSES, cols].bitcast(I32),
+                out=w_codes[gate][:, 1:PASSES, :].bitcast(I32),
                 in_=gru_Whh_words[:, :, cols].rearrange("g p c -> p g c").bitcast(I32),
             )
 
@@ -139,13 +142,14 @@ def tile_rssm_pb_kernel(
                         out=x_codes[:, g, cols].bitcast(FP8X4), scales=x_scales[:, g, cols], in_=grouped_tiles[g][:]
                     )
 
-            def spread_biases():
+            def repeat_z_biases():
                 for half in range(HALVES):
                     cols = slice(BANK * half, BANK * (half + 1))
                     repeated = psum.tile([P, BANK], F32, tag="update")
                     nc.tensor.matmul(repeated[:], lhsT=z_rows_only[:], rhs=bias_rows[:, cols], start=True, stop=True)
                     nc.scalar.copy(out=bias_z[:, cols], in_=repeated[:])
-                nc.vector.tensor_copy(out=bias_rows_f32[:], in_=bias_rows[:])
+
+            def turn_biases():
                 for half in range(HALVES):
                     units = slice(TILES_PER_HALF * half, TILES_PER_HALF * (half + 1))
                     turned = psum.tile([P, TILES_PER_HALF, P], F32, tag="flipped")
@@ -166,7 +170,7 @@ def tile_rssm_pb_kernel(
                             out=update[:],
                             lhsT=x_codes[:, g, rows].bitcast(FP8X4),
                             lhsT_scale=x_scales[:, g, rows],
-                            rhs=w_codes[:, g, 2 * first : 2 * (first + BANK)].bitcast(FP4X4),
+                            rhs=w_codes[GATE_Z][:, g, 2 * BANK * half : 2 * BANK * (half + 1)].bitcast(FP4X4),
                             rhs_scale=w_scales[:, g, first : first + BANK],
                             start=(g == 0),
                             stop=(g == PASSES - 1),
@@ -181,7 +185,8 @@ def tile_rssm_pb_kernel(
                     )
 
             quantise_pair(0)
-            spread_biases()
+            repeat_z_biases()
+            turn_biases()
             for pair in range(PAIRS):
                 update_gate(2 * pair)
                 if pair + 1 < PAIRS:
@@ -195,7 +200,7 @@ def tile_rssm_pb_kernel(
                 cols = slice(BANK * half, BANK * (half + 1))
                 nc.tensor.matmul_mx(
                     out=acc[:],
-                    lhsT=w_codes[:, g, 2 * first : 2 * (first + P)].bitcast(FP4X4),
+                    lhsT=w_codes[gate][:, g, 2 * P * j : 2 * P * (j + 1)].bitcast(FP4X4),
                     lhsT_scale=w_scales[:, g, first : first + P],
                     rhs=x_codes[:, g, cols].bitcast(FP8X4),
                     rhs_scale=x_scales[:, g, cols],

@@ -86,9 +86,9 @@ def tile_rssm_pb_kernel(
 
         def load_pair(pair):
             tiles = slice(2 * pair, 2 * pair + 2)
-            nc.sync.dma_start(out=x_rows[:, tiles, XG:], in_=state_rows[:, tiles, :])
             nc.sync.dma_start(out=x_rows[:, tiles, 0:LATENT], in_=sample_rows[:, tiles, :])
             nc.sync.dma_start(out=x_rows[:, tiles, LATENT:XG], in_=action_rows[:, tiles, :])
+            nc.sync.dma_start(out=x_rows[:, tiles, XG:], in_=state_rows[:, tiles, :])
 
         def load_gate_codes(gate):
             cols = slice(2 * HIDDEN * gate, 2 * HIDDEN * (gate + 1))
@@ -131,10 +131,7 @@ def tile_rssm_pb_kernel(
                             )
                     grouped = work.tile([P, 2 * K_PASS], BF16, align_bytes=64)
                     grouped_words = grouped[:].bitcast(F32).rearrange("p (h b u) -> p h b u", h=2, u=2)
-                    if (PASSES * pair + g) % 2 == 0:
-                        nc.vector.tensor_copy(out=grouped_words, in_=flipped[:].rearrange("p h u b -> p h b u"))
-                    else:
-                        nc.scalar.copy(out=grouped_words, in_=flipped[:].rearrange("p h u b -> p h b u"))
+                    nc.scalar.copy(out=grouped_words, in_=flipped[:].rearrange("p h u b -> p h b u"))
                     grouped_tiles.append(grouped)
                 cols = slice(2 * P * pair, 2 * P * (pair + 1))
                 for g in range(PASSES):
@@ -185,8 +182,8 @@ def tile_rssm_pb_kernel(
                     )
 
             quantise_pair(0)
-            repeat_z_biases()
             turn_biases()
+            repeat_z_biases()
             for pair in range(PAIRS):
                 update_gate(2 * pair)
                 if pair + 1 < PAIRS:
@@ -251,7 +248,7 @@ def tile_rssm_pb_kernel(
                     news.append(new)
                 return news, fresh
 
-            def blend_and_store(j, news, fresh):
+            def blend_and_store(j, news, fresh, adder):
                 cols = slice(P * j, P * (j + 1))
                 new_rows = []
                 for half in range(HALVES):
@@ -259,16 +256,22 @@ def tile_rssm_pb_kernel(
                     for c in range(TILES_PER_HALF):
                         nc.tensor.transpose(turned[:, c, :], news[half][:, P * c : P * (c + 1)], identity[:])
                     new_rows.append(turned)
+                beliefs = []
                 for half in range(HALVES):
                     tiles = slice(TILES_PER_HALF * half, TILES_PER_HALF * (half + 1))
                     belief = work.tile([P, TILES_PER_HALF, P], F32)
                     nc.vector.tensor_tensor(out=belief[:], in0=new_rows[half][:], in1=fresh[:, tiles, :], op=ALU.mult)
-                    nc.gpsimd.tensor_tensor(out=belief[:], in0=belief[:], in1=carried[:, tiles, cols], op=ALU.add)
-                    nc.sync.dma_start(out=out_rows[:, tiles, cols], in_=belief[:])
+                    beliefs.append(belief)
+                for half in range(HALVES):
+                    tiles = slice(TILES_PER_HALF * half, TILES_PER_HALF * (half + 1))
+                    adder.tensor_tensor(
+                        out=beliefs[half][:], in0=beliefs[half][:], in1=carried[:, tiles, cols], op=ALU.add
+                    )
+                    nc.sync.dma_start(out=out_rows[:, tiles, cols], in_=beliefs[half][:])
 
             waiting = candidate(0)
             for j in range(1, UNITS):
                 following = candidate(j)
-                blend_and_store(j - 1, waiting[0], waiting[1])
+                blend_and_store(j - 1, waiting[0], waiting[1], nc.gpsimd)
                 waiting = following
-            blend_and_store(UNITS - 1, waiting[0], waiting[1])
+            blend_and_store(UNITS - 1, waiting[0], waiting[1], nc.vector)

@@ -131,7 +131,10 @@ def tile_rssm_pb_kernel(
                             )
                     grouped = work.tile([P, 2 * K_PASS], BF16, align_bytes=64)
                     grouped_words = grouped[:].bitcast(F32).rearrange("p (h b u) -> p h b u", h=2, u=2)
-                    nc.scalar.copy(out=grouped_words, in_=flipped[:].rearrange("p h u b -> p h b u"))
+                    if (PASSES * pair + g) % 2 == 0:
+                        nc.vector.tensor_copy(out=grouped_words, in_=flipped[:].rearrange("p h u b -> p h b u"))
+                    else:
+                        nc.scalar.copy(out=grouped_words, in_=flipped[:].rearrange("p h u b -> p h b u"))
                     grouped_tiles.append(grouped)
                 cols = slice(2 * P * pair, 2 * P * (pair + 1))
                 for g in range(PASSES):
@@ -182,8 +185,8 @@ def tile_rssm_pb_kernel(
                     )
 
             quantise_pair(0)
-            turn_biases()
             repeat_z_biases()
+            turn_biases()
             for pair in range(PAIRS):
                 update_gate(2 * pair)
                 if pair + 1 < PAIRS:

@@ -51,14 +51,21 @@ def tile_rssm_pb_kernel(
         resident = ctx.enter_context(tc.tile_pool(name="resident", bufs=1))
         work = ctx.enter_context(tc.tile_pool(name="work", bufs=4))
 
-        x_rows = resident.tile([P, TILES, XG + HIDDEN], BF16)
-        x_words = x_rows[:].bitcast(F32)
+        xg_rows = resident.tile([P, TILES, XG], BF16)
+        state_rows = resident.tile([P, TILES, HIDDEN], BF16)
+        pass_words = [
+            xg_rows[:].bitcast(F32),
+            state_rows[:].bitcast(F32)[:, :, 0:WORDS],
+            state_rows[:].bitcast(F32)[:, :, WORDS : 2 * WORDS],
+        ]
         x_codes = resident.tile([P, PASSES, BATCH], U32, align_bytes=64)
         x_scales = resident.tile([P, PASSES, BATCH], U8, align_bytes=64)
         w_codes = [
             resident.tile([P, PASSES, 2 * HIDDEN], U8, align_bytes=64, name="w_codes_%d" % gate) for gate in range(3)
         ]
-        w_scales = resident.tile([P, PASSES, 3 * HIDDEN], U8, align_bytes=64)
+        w_scales = [
+            resident.tile([P, PASSES, HIDDEN], U8, align_bytes=64, name="w_scales_%d" % gate) for gate in range(3)
+        ]
         z_pre = resident.tile([P, TILES, HIDDEN], F32)
         carried = resident.tile([P, TILES, HIDDEN], F32)
         identity = resident.tile([P, P], F32)
@@ -69,78 +76,106 @@ def tile_rssm_pb_kernel(
         bias_cols = resident.tile([P, UNITS, P], F32)
         bias_r = resident.tile([P, UNITS, 1], F32)
 
-        nc.vector.memset(bias_rows[:], 0.0)
-        nc.vector.memset(w_scales[:].bitcast(I32), 0)
+        nc.vector.memset(w_scales[GATE_Z][:].bitcast(I32), 0)
+        nc.vector.memset(bias_rows[:].bitcast(I32), 0)
         nc.vector.memset(z_rows_only[:], 0.0)
         nc.vector.memset(z_rows_only[32:64, :], 1.0)
+        nc.vector.memset(w_scales[GATE_R][:].bitcast(I32), 0)
+        nc.vector.memset(w_scales[GATE_N][:].bitcast(I32), 0)
         make_identity(nc, identity[:])
+        table_probe = resident.tile([P, 1], F32)
+        nc.scalar.activation(out=table_probe[:], in_=z_rows_only[:, 0:1], func=ACT.Sigmoid)
 
-        nc.scalar.dma_start(out=bias_rows[0:96:32, :], in_=gru_bih.rearrange("(g n) -> g n", g=3))
-        nc.scalar.dma_start(out=bias_rows[1:97:32, :], in_=gru_bhh.rearrange("(g n) -> g n", g=3))
-        nc.vector.tensor_copy(out=bias_rows_f32[:], in_=bias_rows[:])
+        nc.gpsimd.dma_start(out=bias_rows[0:96:32, :], in_=gru_bih.rearrange("(g n) -> g n", g=3))
+        nc.gpsimd.dma_start(out=bias_rows[1:97:32, :], in_=gru_bhh.rearrange("(g n) -> g n", g=3))
 
-        sample_rows = sample.rearrange("(p i) c -> p i c", i=TILES)
-        action_rows = prev_action.rearrange("(p i) c -> p i c", i=TILES)
-        state_rows = prev_state.rearrange("(p i) c -> p i c", i=TILES)
+        sample_dram = sample.rearrange("(p i) c -> p i c", i=TILES)
+        action_dram = prev_action.rearrange("(p i) c -> p i c", i=TILES)
+        state_dram = prev_state.rearrange("(p i) c -> p i c", i=TILES)
         out_rows = out.rearrange("(p i) h -> p i h", i=TILES)
 
-        def load_pair(pair):
+        def load_xg(pair):
             tiles = slice(2 * pair, 2 * pair + 2)
-            nc.sync.dma_start(out=x_rows[:, tiles, 0:LATENT], in_=sample_rows[:, tiles, :])
-            nc.sync.dma_start(out=x_rows[:, tiles, LATENT:XG], in_=action_rows[:, tiles, :])
-            nc.sync.dma_start(out=x_rows[:, tiles, XG:], in_=state_rows[:, tiles, :])
+            nc.sync.dma_start(out=xg_rows[:, tiles, 0:LATENT], in_=sample_dram[:, tiles, :])
+            nc.sync.dma_start(out=xg_rows[:, tiles, LATENT:XG], in_=action_dram[:, tiles, :])
 
-        def load_gate_codes(gate):
+        def load_state(pair):
+            tiles = slice(2 * pair, 2 * pair + 2)
+            nc.sync.dma_start(out=state_rows[:, tiles, :], in_=state_dram[:, tiles, :])
+
+        def load_input_codes(gate):
             cols = slice(2 * HIDDEN * gate, 2 * HIDDEN * (gate + 1))
             nc.sync.dma_start(out=w_codes[gate][:, 0, :].bitcast(I32), in_=gru_Wih_words[0, :, cols].bitcast(I32))
+
+        def load_state_codes(gate):
+            cols = slice(2 * HIDDEN * gate, 2 * HIDDEN * (gate + 1))
             nc.sync.dma_start(
                 out=w_codes[gate][:, 1:PASSES, :].bitcast(I32),
                 in_=gru_Whh_words[:, :, cols].rearrange("g p c -> p g c").bitcast(I32),
             )
 
-        def load_scales():
+        def load_input_scales(gate):
+            cols = slice(HIDDEN * gate, HIDDEN * (gate + 1))
             for s in range(4):
                 nc.sync.dma_start(
-                    out=w_scales[s:P:32, 0, :].bitcast(I32), in_=gru_Wih_scales[0, s:16:4, :].bitcast(I32)
-                )
-                nc.sync.dma_start(
-                    out=w_scales[s:P:32, 1:PASSES, :].bitcast(I32),
-                    in_=gru_Whh_scales[:, s:16:4, :].rearrange("g q n -> q g n").bitcast(I32),
+                    out=w_scales[gate][s:P:32, 0, :].bitcast(I32), in_=gru_Wih_scales[0, s:16:4, cols].bitcast(I32)
                 )
 
-        load_pair(0)
-        load_gate_codes(GATE_Z)
-        load_scales()
-        for pair in range(1, PAIRS):
-            load_pair(pair)
-        load_gate_codes(GATE_R)
-        load_gate_codes(GATE_N)
+        def load_state_scales(gate):
+            cols = slice(HIDDEN * gate, HIDDEN * (gate + 1))
+            for s in range(4):
+                nc.sync.dma_start(
+                    out=w_scales[gate][s:P:32, 1:PASSES, :].bitcast(I32),
+                    in_=gru_Whh_scales[:, s:16:4, cols].rearrange("g q n -> q g n").bitcast(I32),
+                )
+
+        for pair in range(0, 2):
+            load_xg(pair)
+            load_state(pair)
+        load_input_scales(GATE_Z)
+        load_state_scales(GATE_Z)
+        load_input_codes(GATE_Z)
+        load_state_codes(GATE_Z)
+        for pair in range(2, PAIRS):
+            load_xg(pair)
+            load_state(pair)
+        for gate in (GATE_R, GATE_N):
+            load_input_codes(gate)
+            load_state_codes(gate)
+            load_input_scales(gate)
+            load_state_scales(gate)
 
         with tc.psum_pool(name="psum_update", bufs=4, reuse_waits="tile") as psum:
+
+            def flip(pair, g, copier):
+                flipped = psum.tile([P, 2, 2, P], F32, tag="flipped")
+                for h in range(2):
+                    for u in range(2):
+                        nc.tensor.transpose(
+                            flipped[:, h, u, :],
+                            pass_words[g][:, 2 * pair + h, u:WORDS:2],
+                            identity[:],
+                        )
+                grouped = work.tile([P, 2 * K_PASS], BF16, align_bytes=64)
+                copier(
+                    out=grouped[:].bitcast(F32).rearrange("p (h b u) -> p h b u", h=2, u=2),
+                    in_=flipped[:].rearrange("p h u b -> p h b u"),
+                )
+                return grouped
+
+            def quantise(pair, g, grouped):
+                cols = slice(2 * P * pair, 2 * P * (pair + 1))
+                nc.vector.quantize_mx(
+                    out=x_codes[:, g, cols].bitcast(FP8X4), scales=x_scales[:, g, cols], in_=grouped[:]
+                )
 
             def quantise_pair(pair):
                 grouped_tiles = []
                 for g in range(PASSES):
-                    flipped = psum.tile([P, 2, 2, P], F32, tag="flipped")
-                    for h in range(2):
-                        for u in range(2):
-                            nc.tensor.transpose(
-                                flipped[:, h, u, :],
-                                x_words[:, 2 * pair + h, WORDS * g + u : WORDS * (g + 1) : 2],
-                                identity[:],
-                            )
-                    grouped = work.tile([P, 2 * K_PASS], BF16, align_bytes=64)
-                    grouped_words = grouped[:].bitcast(F32).rearrange("p (h b u) -> p h b u", h=2, u=2)
-                    if (PASSES * pair + g) % 2 == 0:
-                        nc.vector.tensor_copy(out=grouped_words, in_=flipped[:].rearrange("p h u b -> p h b u"))
-                    else:
-                        nc.scalar.copy(out=grouped_words, in_=flipped[:].rearrange("p h u b -> p h b u"))
-                    grouped_tiles.append(grouped)
-                cols = slice(2 * P * pair, 2 * P * (pair + 1))
+                    even = (PASSES * pair + g) % 2 == 0
+                    grouped_tiles.append(flip(pair, g, nc.vector.tensor_copy if even else nc.scalar.copy))
                 for g in range(PASSES):
-                    nc.vector.quantize_mx(
-                        out=x_codes[:, g, cols].bitcast(FP8X4), scales=x_scales[:, g, cols], in_=grouped_tiles[g][:]
-                    )
+                    quantise(pair, g, grouped_tiles[g])
 
             def repeat_z_biases():
                 for half in range(HALVES):
@@ -159,49 +194,59 @@ def tile_rssm_pb_kernel(
                     nc.scalar.copy(out=bias_cols[:, units, :], in_=turned[:])
                 nc.vector.tensor_tensor(out=bias_r[:], in0=bias_cols[:, :, 0:1], in1=bias_cols[:, :, 1:2], op=ALU.add)
 
-            def update_gate(i):
+            def open_update():
+                return [psum.tile([P, BANK], F32, tag="update", name="update") for half in range(HALVES)]
+
+            def update_passes(i, banks, g):
                 rows = slice(P * i, P * (i + 1))
                 for half in range(HALVES):
+                    nc.tensor.matmul_mx(
+                        out=banks[half][:],
+                        lhsT=x_codes[:, g, rows].bitcast(FP8X4),
+                        lhsT_scale=x_scales[:, g, rows],
+                        rhs=w_codes[GATE_Z][:, g, 2 * BANK * half : 2 * BANK * (half + 1)].bitcast(FP4X4),
+                        rhs_scale=w_scales[GATE_Z][:, g, BANK * half : BANK * (half + 1)],
+                        start=(g == 0),
+                        stop=(g == PASSES - 1),
+                    )
+
+            def finish_update(i, banks):
+                for half in range(HALVES):
                     cols = slice(BANK * half, BANK * (half + 1))
-                    first = GATE_Z * HIDDEN + BANK * half
-                    update = psum.tile([P, BANK], F32, tag="update")
-                    for g in range(PASSES):
-                        nc.tensor.matmul_mx(
-                            out=update[:],
-                            lhsT=x_codes[:, g, rows].bitcast(FP8X4),
-                            lhsT_scale=x_scales[:, g, rows],
-                            rhs=w_codes[GATE_Z][:, g, 2 * BANK * half : 2 * BANK * (half + 1)].bitcast(FP4X4),
-                            rhs_scale=w_scales[:, g, first : first + BANK],
-                            start=(g == 0),
-                            stop=(g == PASSES - 1),
-                        )
-                    nc.vector.tensor_tensor(out=z_pre[:, i, cols], in0=update[:], in1=bias_z[:, cols], op=ALU.add)
+                    nc.vector.tensor_tensor(out=z_pre[:, i, cols], in0=banks[half][:], in1=bias_z[:, cols], op=ALU.add)
                     nc.scalar.activation(out=carried[:, i, cols], in_=z_pre[:, i, cols], func=ACT.Sigmoid)
                     nc.gpsimd.tensor_tensor(
                         out=carried[:, i, cols],
                         in0=carried[:, i, cols],
-                        in1=x_rows[:, i, XG + BANK * half : XG + BANK * (half + 1)],
+                        in1=state_rows[:, i, cols],
                         op=ALU.mult,
                     )
 
+            def update_gate(i):
+                banks = open_update()
+                for g in range(PASSES):
+                    update_passes(i, banks, g)
+                finish_update(i, banks)
+
             quantise_pair(0)
+            nc.vector.tensor_copy(out=bias_rows_f32[:], in_=bias_rows[:])
+            quantise_pair(1)
             repeat_z_biases()
             turn_biases()
             for pair in range(PAIRS):
                 update_gate(2 * pair)
-                if pair + 1 < PAIRS:
-                    quantise_pair(pair + 1)
                 update_gate(2 * pair + 1)
+                if pair + 2 < PAIRS:
+                    quantise_pair(pair + 2)
 
         with tc.psum_pool(name="psum_candidate", bufs=2, reuse_waits="tile") as psum:
 
             def weights_stationary(acc, gate, j, g, half, start, stop):
-                first = gate * HIDDEN + P * j
                 cols = slice(BANK * half, BANK * (half + 1))
                 nc.tensor.matmul_mx(
                     out=acc[:],
                     lhsT=w_codes[gate][:, g, 2 * P * j : 2 * P * (j + 1)].bitcast(FP4X4),
-                    lhsT_scale=w_scales[:, g, first : first + P],
+                    lhsT_scale=w_scales[gate][:, g, P * j : P * (j + 1)],
                     rhs=x_codes[:, g, cols].bitcast(FP8X4),
                     rhs_scale=x_scales[:, g, cols],
                     start=start,

@@ -50,6 +50,7 @@ def tile_rssm_pb_kernel(
         ctx.enter_context(tc.manual_schedule())
         resident = ctx.enter_context(tc.tile_pool(name="resident", bufs=1))
         work = ctx.enter_context(tc.tile_pool(name="work", bufs=4))
+        outgoing = ctx.enter_context(tc.tile_pool(name="outgoing", bufs=8))
 
         xg_rows = resident.tile([P, TILES, XG], BF16)
         state_rows = resident.tile([P, TILES, HIDDEN], BF16)
@@ -69,25 +70,24 @@ def tile_rssm_pb_kernel(
         z_pre = resident.tile([P, TILES, HIDDEN], F32)
         carried = resident.tile([P, TILES, HIDDEN], F32)
         identity = resident.tile([P, P], F32)
-        bias_rows = resident.tile([P, HIDDEN], BF16)
-        bias_rows_f32 = resident.tile([P, HIDDEN], F32)
-        z_rows_only = resident.tile([P, P], BF16)
+        bias_rows = resident.tile([P, P], BF16)
+        bias_rows_f32 = resident.tile([P, P], F32)
+        z_rows = resident.tile([P, UNITS], BF16)
         bias_z = resident.tile([P, HIDDEN], F32)
-        bias_cols = resident.tile([P, UNITS, P], F32)
-        bias_r = resident.tile([P, UNITS, 1], F32)
+        bias_cols = resident.tile([P, P], F32)
+        bias_r = resident.tile([P, UNITS], F32)
 
-        nc.vector.memset(w_scales[GATE_Z][:].bitcast(I32), 0)
         nc.vector.memset(bias_rows[:].bitcast(I32), 0)
-        nc.vector.memset(z_rows_only[:], 0.0)
-        nc.vector.memset(z_rows_only[32:64, :], 1.0)
+        nc.vector.memset(w_scales[GATE_Z][:].bitcast(I32), 0)
         nc.vector.memset(w_scales[GATE_R][:].bitcast(I32), 0)
         nc.vector.memset(w_scales[GATE_N][:].bitcast(I32), 0)
         make_identity(nc, identity[:])
+        z_bih, z_bhh = UNITS * GATE_Z, 32 + UNITS * GATE_Z
+        nc.vector.tensor_tensor(
+            out=z_rows[:], in0=identity[:, z_bih : z_bih + UNITS], in1=identity[:, z_bhh : z_bhh + UNITS], op=ALU.add
+        )
         table_probe = resident.tile([P, 1], F32)
-        nc.scalar.activation(out=table_probe[:], in_=z_rows_only[:, 0:1], func=ACT.Sigmoid)
-
-        nc.gpsimd.dma_start(out=bias_rows[0:96:32, :], in_=gru_bih.rearrange("(g n) -> g n", g=3))
-        nc.gpsimd.dma_start(out=bias_rows[1:97:32, :], in_=gru_bhh.rearrange("(g n) -> g n", g=3))
+        nc.scalar.activation(out=table_probe[:], in_=bias_rows[:, 0:1], func=ACT.Sigmoid)
 
         sample_dram = sample.rearrange("(p i) c -> p i c", i=TILES)
         action_dram = prev_action.rearrange("(p i) c -> p i c", i=TILES)
@@ -132,6 +132,8 @@ def tile_rssm_pb_kernel(
         for pair in range(0, 2):
             load_xg(pair)
             load_state(pair)
+        nc.gpsimd.dma_start(out=bias_rows[0 : 3 * UNITS, :], in_=gru_bih.rearrange("(r c) -> r c", c=P))
+        nc.gpsimd.dma_start(out=bias_rows[32 : 32 + 3 * UNITS, :], in_=gru_bhh.rearrange("(r c) -> r c", c=P))
         load_input_scales(GATE_Z)
         load_state_scales(GATE_Z)
         load_input_codes(GATE_Z)
@@ -179,20 +181,30 @@ def tile_rssm_pb_kernel(
 
             def repeat_z_biases():
                 for half in range(HALVES):
-                    cols = slice(BANK * half, BANK * (half + 1))
-                    repeated = psum.tile([P, BANK], F32, tag="update")
-                    nc.tensor.matmul(repeated[:], lhsT=z_rows_only[:], rhs=bias_rows[:, cols], start=True, stop=True)
-                    nc.scalar.copy(out=bias_z[:, cols], in_=repeated[:])
-
-            def turn_biases():
-                for half in range(HALVES):
-                    units = slice(TILES_PER_HALF * half, TILES_PER_HALF * (half + 1))
-                    turned = psum.tile([P, TILES_PER_HALF, P], F32, tag="flipped")
+                    repeated = psum.tile([P, TILES_PER_HALF, P], F32, tag="update")
                     for c in range(TILES_PER_HALF):
                         j = TILES_PER_HALF * half + c
-                        nc.tensor.transpose(turned[:, c, :], bias_rows_f32[:, P * j : P * (j + 1)], identity[:])
-                    nc.scalar.copy(out=bias_cols[:, units, :], in_=turned[:])
-                nc.vector.tensor_tensor(out=bias_r[:], in0=bias_cols[:, :, 0:1], in1=bias_cols[:, :, 1:2], op=ALU.add)
+                        nc.tensor.matmul(
+                            repeated[:, c, :],
+                            lhsT=z_rows[:, j : j + 1].to_broadcast([P, P]),
+                            rhs=bias_rows[:],
+                            start=True,
+                            stop=True,
+                        )
+                    nc.scalar.copy(
+                        out=bias_z[:, BANK * half : BANK * (half + 1)], in_=repeated[:].rearrange("p c n -> p (c n)")
+                    )
+
+            def turn_biases():
+                turned = psum.tile([P, P], F32, tag="flipped")
+                nc.tensor.transpose(turned[:], bias_rows_f32[:], identity[:])
+                nc.scalar.copy(out=bias_cols[:], in_=turned[:])
+
+            def add_reset_biases():
+                r_bih, r_bhh = UNITS * GATE_R, 32 + UNITS * GATE_R
+                nc.vector.tensor_tensor(
+                    out=bias_r[:], in0=bias_cols[:, r_bih : r_bih + UNITS], in1=bias_cols[:, r_bhh : r_bhh + UNITS], op=ALU.add
+                )
 
             def open_update():
                 return [psum.tile([P, BANK], F32, tag="update", name="update") for half in range(HALVES)]
@@ -236,6 +248,8 @@ def tile_rssm_pb_kernel(
             for pair in range(PAIRS):
                 update_gate(2 * pair)
                 update_gate(2 * pair + 1)
+                if pair == 0:
+                    add_reset_biases()
                 if pair + 2 < PAIRS:
                     quantise_pair(pair + 2)
 
@@ -253,73 +267,151 @@ def tile_rssm_pb_kernel(
                     stop=stop,
                 )
 
-            def candidate(j):
-                reset_sums, state_sums, input_sums = [], [], []
-                for half in range(HALVES):
-                    reset_sum = psum.tile([P, BANK], F32)
-                    for g in range(PASSES):
-                        weights_stationary(reset_sum, GATE_R, j, g, half, start=(g == 0), stop=(g == PASSES - 1))
-                    reset_sums.append(reset_sum)
-                for half in range(HALVES):
-                    state_sum = psum.tile([P, BANK], F32)
-                    for g in range(1, PASSES):
-                        weights_stationary(state_sum, GATE_N, j, g, half, start=(g == 1), stop=(g == PASSES - 1))
-                    state_sums.append(state_sum)
-                    input_sum = psum.tile([P, BANK], F32)
-                    weights_stationary(input_sum, GATE_N, j, 0, half, start=True, stop=True)
-                    input_sums.append(input_sum)
+            def reset_passes(j, half):
+                reset_sum = psum.tile([P, BANK], F32)
+                for g in range(PASSES):
+                    weights_stationary(reset_sum, GATE_R, j, g, half, start=(g == 0), stop=(g == PASSES - 1))
+                return reset_sum
 
-                inner = []
-                for half in range(HALVES):
-                    reset = work.tile([P, BANK], F32)
-                    nc.scalar.activation(out=reset[:], in_=reset_sums[half][:], func=ACT.Sigmoid, bias=bias_r[:, j, :])
-                    gated = work.tile([P, BANK], F32)
-                    nc.vector.scalar_tensor_tensor(
-                        out=gated[:],
-                        in0=state_sums[half][:],
-                        scalar=bias_cols[:, j, 65:66],
-                        in1=reset[:],
-                        op0=ALU.add,
-                        op1=ALU.mult,
-                    )
-                    inner.append(gated)
-                for half in range(HALVES):
-                    nc.vector.tensor_tensor(out=inner[half][:], in0=inner[half][:], in1=input_sums[half][:], op=ALU.add)
+            def state_passes(j, half):
+                state_sum = psum.tile([P, BANK], F32)
+                for g in range(1, PASSES):
+                    weights_stationary(state_sum, GATE_N, j, g, half, start=(g == 1), stop=(g == PASSES - 1))
+                return state_sum
 
+            def input_pass(j, half):
+                input_sum = psum.tile([P, BANK], F32)
+                weights_stationary(input_sum, GATE_N, j, 0, half, start=True, stop=True)
+                return input_sum
+
+            def reset_gate(j, reset_sum):
+                reset = work.tile([P, BANK], F32)
+                nc.scalar.activation(out=reset[:], in_=reset_sum[:], func=ACT.Sigmoid, bias=bias_r[:, j : j + 1])
+                return reset
+
+            def gate_state(j, state_sum, reset):
+                n_bhh = 32 + UNITS * GATE_N + j
+                gated = work.tile([P, BANK], F32)
+                nc.vector.scalar_tensor_tensor(
+                    out=gated[:],
+                    in0=state_sum[:],
+                    scalar=bias_cols[:, n_bhh : n_bhh + 1],
+                    in1=reset[:],
+                    op0=ALU.add,
+                    op1=ALU.mult,
+                )
+                return gated
+
+            def add_input(gated, input_sum, cols):
+                nc.vector.tensor_tensor(out=gated[:, cols], in0=gated[:, cols], in1=input_sum[:, cols], op=ALU.add)
+
+            def fresh_share(j):
                 fresh = work.tile([P, TILES, P], F32)
                 nc.scalar.activation(out=fresh[:], in_=z_pre[:, :, P * j : P * (j + 1)], func=ACT.Sigmoid, scale=-1.0)
+                return fresh
 
+            def candidate_values(j, gated, new, cols):
+                n_bih = UNITS * GATE_N + j
+                nc.scalar.activation(
+                    out=new[:, cols], in_=gated[:, cols], func=ACT.Tanh, bias=bias_cols[:, n_bih : n_bih + 1]
+                )
+
+            def candidate(j):
+                reset_sums = [reset_passes(j, half) for half in range(HALVES)]
+                state_sums = [state_passes(j, half) for half in range(HALVES)]
+                input_sums = [input_pass(j, half) for half in range(HALVES)]
+                inner = []
+                for half in range(HALVES):
+                    inner.append(gate_state(j, state_sums[half], reset_gate(j, reset_sums[half])))
+                for half in range(HALVES):
+                    add_input(inner[half], input_sums[half], slice(0, BANK))
+                fresh = fresh_share(j)
                 news = []
                 for half in range(HALVES):
                     new = work.tile([P, BANK], F32)
-                    nc.scalar.activation(out=new[:], in_=inner[half][:], func=ACT.Tanh, bias=bias_cols[:, j, 64:65])
+                    candidate_values(j, inner[half], new, slice(0, BANK))
                     news.append(new)
                 return news, fresh
 
-            def blend_and_store(j, news, fresh, adder):
+            def turn(turned, new, first, count):
+                for c in range(count):
+                    nc.tensor.transpose(turned[:, c, :], new[:, P * (first + c) : P * (first + c + 1)], identity[:])
+
+            def scale_new(turned, fresh, tiles):
+                belief = outgoing.tile([P, TILES_PER_HALF, P], F32)
+                count = tiles.stop - tiles.start
+                nc.vector.tensor_tensor(
+                    out=belief[:, 0:count, :], in0=turned[:, 0:count, :], in1=fresh[:, tiles, :], op=ALU.mult
+                )
+                return belief
+
+            def add_and_store(j, belief, tiles, adder):
                 cols = slice(P * j, P * (j + 1))
-                new_rows = []
+                count = tiles.stop - tiles.start
+                adder.tensor_tensor(
+                    out=belief[:, 0:count, :], in0=belief[:, 0:count, :], in1=carried[:, tiles, cols], op=ALU.add
+                )
+                nc.sync.dma_start(out=out_rows[:, tiles, cols], in_=belief[:, 0:count, :])
+
+            def half_tiles(half):
+                return slice(TILES_PER_HALF * half, TILES_PER_HALF * (half + 1))
+
+            def turn_unit(news):
+                turned_halves = []
                 for half in range(HALVES):
                     turned = psum.tile([P, TILES_PER_HALF, P], F32)
-                    for c in range(TILES_PER_HALF):
-                        nc.tensor.transpose(turned[:, c, :], news[half][:, P * c : P * (c + 1)], identity[:])
-                    new_rows.append(turned)
-                beliefs = []
+                    turn(turned, news[half], 0, TILES_PER_HALF)
+                    turned_halves.append(turned)
+                return turned_halves
+
+            def blend_and_store(j, news, fresh):
+                turned_halves = turn_unit(news)
+                beliefs = [scale_new(turned_halves[half], fresh, half_tiles(half)) for half in range(HALVES)]
                 for half in range(HALVES):
-                    tiles = slice(TILES_PER_HALF * half, TILES_PER_HALF * (half + 1))
-                    belief = work.tile([P, TILES_PER_HALF, P], F32)
-                    nc.vector.tensor_tensor(out=belief[:], in0=new_rows[half][:], in1=fresh[:, tiles, :], op=ALU.mult)
-                    beliefs.append(belief)
-                for half in range(HALVES):
-                    tiles = slice(TILES_PER_HALF * half, TILES_PER_HALF * (half + 1))
-                    adder.tensor_tensor(
-                        out=beliefs[half][:], in0=beliefs[half][:], in1=carried[:, tiles, cols], op=ALU.add
-                    )
-                    nc.sync.dma_start(out=out_rows[:, tiles, cols], in_=beliefs[half][:])
+                    add_and_store(j, beliefs[half], half_tiles(half), nc.gpsimd)
 
             waiting = candidate(0)
-            for j in range(1, UNITS):
+            for j in range(1, UNITS - 1):
                 following = candidate(j)
-                blend_and_store(j - 1, waiting[0], waiting[1], nc.gpsimd)
+                blend_and_store(j - 1, waiting[0], waiting[1])
                 waiting = following
-            blend_and_store(UNITS - 1, waiting[0], waiting[1], nc.vector)
+
+            last = UNITS - 1
+            whole = slice(0, BANK)
+            pieces = [slice(0, BANK // 2), slice(BANK // 2, BANK)]
+            news, fresh = waiting
+            reset_sum = reset_passes(last, 0)
+            state_sum = state_passes(last, 0)
+            input_sum = input_pass(last, 0)
+            gated = gate_state(last, state_sum, reset_gate(last, reset_sum))
+            add_input(gated, input_sum, whole)
+            last_fresh = fresh_share(last)
+            reset_sum = reset_passes(last, 1)
+            turned_halves = turn_unit(news)
+            reset = reset_gate(last, reset_sum)
+            first_new = work.tile([P, BANK], F32, name="new")
+            candidate_values(last, gated, first_new, whole)
+            state_sum = state_passes(last, 1)
+            input_sum = input_pass(last, 1)
+            for half in range(HALVES):
+                add_and_store(last - 1, scale_new(turned_halves[half], fresh, half_tiles(half)), half_tiles(half), nc.gpsimd)
+            gated = gate_state(last, state_sum, reset)
+            second_new = work.tile([P, BANK], F32, name="new")
+            for piece in pieces:
+                add_input(gated, input_sum, piece)
+                candidate_values(last, gated, second_new, piece)
+            turned = psum.tile([P, TILES_PER_HALF, P], F32)
+            turn(turned, first_new, 0, TILES_PER_HALF)
+            add_and_store(last, scale_new(turned, last_fresh, half_tiles(0)), half_tiles(0), nc.gpsimd)
+            turned_pieces = [
+                psum.tile([P, TILES_PER_HALF, P], F32, tag="turned", name="turned"),
+                psum.tile([P, TILES_PER_HALF, P], F32, tag="reset_sum", name="turned"),
+            ]
+            per_piece = TILES_PER_HALF // 2
+            piece_tiles = [slice(TILES_PER_HALF + per_piece * n, TILES_PER_HALF + per_piece * (n + 1)) for n in range(2)]
+            beliefs = []
+            for n in range(2):
+                turn(turned_pieces[n], second_new, per_piece * n, per_piece)
+                beliefs.append(scale_new(turned_pieces[n], last_fresh, piece_tiles[n]))
+            for n in range(2):
+                add_and_store(last, beliefs[n], piece_tiles[n], nc.vector)

@@ -377,41 +377,18 @@ def tile_rssm_pb_kernel(
                 waiting = following
 
             last = UNITS - 1
-            whole = slice(0, BANK)
-            pieces = [slice(0, BANK // 2), slice(BANK // 2, BANK)]
             news, fresh = waiting
-            reset_sum = reset_passes(last, 0)
-            state_sum = state_passes(last, 0)
-            input_sum = input_pass(last, 0)
-            gated = gate_state(last, state_sum, reset_gate(last, reset_sum))
-            add_input(gated, input_sum, whole)
-            last_fresh = fresh_share(last)
-            reset_sum = reset_passes(last, 1)
+            last_news, last_fresh = candidate(last)
             turned_halves = turn_unit(news)
-            reset = reset_gate(last, reset_sum)
-            first_new = work.tile([P, BANK], F32, name="new")
-            candidate_values(last, gated, first_new, whole)
-            state_sum = state_passes(last, 1)
-            input_sum = input_pass(last, 1)
-            for half in range(HALVES):
-                add_and_store(last - 1, scale_new(turned_halves[half], fresh, half_tiles(half)), half_tiles(half), nc.gpsimd)
-            gated = gate_state(last, state_sum, reset)
-            second_new = work.tile([P, BANK], F32, name="new")
-            for piece in pieces:
-                add_input(gated, input_sum, piece)
-                candidate_values(last, gated, second_new, piece)
-            turned = psum.tile([P, TILES_PER_HALF, P], F32)
-            turn(turned, first_new, 0, TILES_PER_HALF)
-            add_and_store(last, scale_new(turned, last_fresh, half_tiles(0)), half_tiles(0), nc.gpsimd)
-            turned_pieces = [
-                psum.tile([P, TILES_PER_HALF, P], F32, tag="turned", name="turned"),
+            last_turned = [
+                psum.tile([P, TILES_PER_HALF, P], F32, tag="reset_sum", name="turned"),
                 psum.tile([P, TILES_PER_HALF, P], F32, tag="reset_sum", name="turned"),
             ]
-            per_piece = TILES_PER_HALF // 2
-            piece_tiles = [slice(TILES_PER_HALF + per_piece * n, TILES_PER_HALF + per_piece * (n + 1)) for n in range(2)]
-            beliefs = []
-            for n in range(2):
-                turn(turned_pieces[n], second_new, per_piece * n, per_piece)
-                beliefs.append(scale_new(turned_pieces[n], last_fresh, piece_tiles[n]))
-            for n in range(2):
-                add_and_store(last, beliefs[n], piece_tiles[n], nc.vector)
+            for half in range(HALVES):
+                turn(last_turned[half], last_news[half], 0, TILES_PER_HALF)
+            beliefs = [scale_new(turned_halves[half], fresh, half_tiles(half)) for half in range(HALVES)]
+            add_and_store(last - 1, beliefs[0], half_tiles(0), nc.gpsimd)
+            last_beliefs = [scale_new(last_turned[half], last_fresh, half_tiles(half)) for half in range(HALVES)]
+            add_and_store(last - 1, beliefs[1], half_tiles(1), nc.vector)
+            for half in range(HALVES):
+                add_and_store(last, last_beliefs[half], half_tiles(half), nc.vector)

@@ -129,18 +129,20 @@ def tile_rssm_pb_kernel(
                     in_=gru_Whh_scales[:, s:16:4, cols].rearrange("g q n -> q g n").bitcast(I32),
                 )
 
-        for pair in range(0, 2):
-            load_xg(pair)
-            load_state(pair)
         nc.gpsimd.dma_start(out=bias_rows[0 : 3 * UNITS, :], in_=gru_bih.rearrange("(r c) -> r c", c=P))
         nc.gpsimd.dma_start(out=bias_rows[32 : 32 + 3 * UNITS, :], in_=gru_bhh.rearrange("(r c) -> r c", c=P))
+        load_xg(0)
+        load_state(0)
         load_input_scales(GATE_Z)
+        load_xg(1)
+        load_state(1)
         load_state_scales(GATE_Z)
+        load_xg(2)
+        load_state(2)
         load_input_codes(GATE_Z)
         load_state_codes(GATE_Z)
-        for pair in range(2, PAIRS):
-            load_xg(pair)
-            load_state(pair)
+        load_xg(3)
+        load_state(3)
         for gate in (GATE_R, GATE_N):
             load_input_codes(gate)
             load_state_codes(gate)
@@ -243,15 +245,15 @@ def tile_rssm_pb_kernel(
             quantise_pair(0)
             nc.vector.tensor_copy(out=bias_rows_f32[:], in_=bias_rows[:])
             quantise_pair(1)
+            quantise_pair(2)
             repeat_z_biases()
             turn_biases()
-            for pair in range(PAIRS):
-                update_gate(2 * pair)
-                update_gate(2 * pair + 1)
-                if pair == 0:
-                    add_reset_biases()
-                if pair + 2 < PAIRS:
-                    quantise_pair(pair + 2)
+            update_gate(0)
+            update_gate(1)
+            add_reset_biases()
+            quantise_pair(3)
+            for i in range(2, TILES):
+                update_gate(i)
 
         with tc.psum_pool(name="psum_candidate", bufs=2, reuse_waits="tile") as psum:
 

@@ -131,23 +131,14 @@ def tile_rssm_pb_kernel(
 
         nc.gpsimd.dma_start(out=bias_rows[0 : 3 * UNITS, :], in_=gru_bih.rearrange("(r c) -> r c", c=P))
         nc.gpsimd.dma_start(out=bias_rows[32 : 32 + 3 * UNITS, :], in_=gru_bhh.rearrange("(r c) -> r c", c=P))
-        load_xg(0)
-        load_state(0)
-        load_input_scales(GATE_Z)
-        load_xg(1)
-        load_state(1)
-        load_state_scales(GATE_Z)
-        load_xg(2)
-        load_state(2)
-        load_input_codes(GATE_Z)
-        load_state_codes(GATE_Z)
-        load_xg(3)
-        load_state(3)
-        for gate in (GATE_R, GATE_N):
-            load_input_codes(gate)
-            load_state_codes(gate)
+        for pair in range(PAIRS):
+            load_xg(pair)
+            load_state(pair)
+        for gate in (GATE_Z, GATE_R, GATE_N):
             load_input_scales(gate)
+            load_input_codes(gate)
             load_state_scales(gate)
+            load_state_codes(gate)
 
         with tc.psum_pool(name="psum_update", bufs=4, reuse_waits="tile") as psum:
 
@@ -242,16 +233,20 @@ def tile_rssm_pb_kernel(
                     update_passes(i, banks, g)
                 finish_update(i, banks)
 
-            quantise_pair(0)
+            for pair in range(PAIRS - 1):
+                quantise_pair(pair)
             nc.vector.tensor_copy(out=bias_rows_f32[:], in_=bias_rows[:])
-            quantise_pair(1)
-            quantise_pair(2)
+            quantise_pair(PAIRS - 1)
             repeat_z_biases()
             turn_biases()
-            update_gate(0)
-            update_gate(1)
+            first_banks = [open_update(), open_update()]
+            for i in range(2):
+                update_passes(i, first_banks[i], 0)
+            for i in range(2):
+                for g in range(1, PASSES):
+                    update_passes(i, first_banks[i], g)
+                finish_update(i, first_banks[i])
             add_reset_biases()
-            quantise_pair(3)
             for i in range(2, TILES):
                 update_gate(i)
 

@@ -50,7 +50,7 @@ def tile_rssm_pb_kernel(
         ctx.enter_context(tc.manual_schedule())
         resident = ctx.enter_context(tc.tile_pool(name="resident", bufs=1))
         work = ctx.enter_context(tc.tile_pool(name="work", bufs=4))
-        outgoing = ctx.enter_context(tc.tile_pool(name="outgoing", bufs=8))
+        outgoing = ctx.enter_context(tc.tile_pool(name="outgoing", bufs=16))
 
         xg_rows = resident.tile([P, TILES, XG], BF16)
         state_rows = resident.tile([P, TILES, HIDDEN], BF16)
@@ -133,8 +133,13 @@ def tile_rssm_pb_kernel(
         nc.gpsimd.dma_start(out=bias_rows[32 : 32 + 3 * UNITS, :], in_=gru_bhh.rearrange("(r c) -> r c", c=P))
         for pair in range(PAIRS):
             load_xg(pair)
+            if pair == PAIRS - 1:
+                load_input_scales(GATE_Z)
             load_state(pair)
-        for gate in (GATE_Z, GATE_R, GATE_N):
+        load_state_scales(GATE_Z)
+        load_input_codes(GATE_Z)
+        load_state_codes(GATE_Z)
+        for gate in (GATE_R, GATE_N):
             load_input_scales(gate)
             load_input_codes(gate)
             load_state_scales(gate)
@@ -239,13 +244,8 @@ def tile_rssm_pb_kernel(
             quantise_pair(PAIRS - 1)
             repeat_z_biases()
             turn_biases()
-            first_banks = [open_update(), open_update()]
-            for i in range(2):
-                update_passes(i, first_banks[i], 0)
-            for i in range(2):
-                for g in range(1, PASSES):
-                    update_passes(i, first_banks[i], g)
-                finish_update(i, first_banks[i])
+            update_gate(0)
+            update_gate(1)
             add_reset_biases()
             for i in range(2, TILES):
                 update_gate(i)

from contextlib import ExitStack

import concourse.mybir as mybir
from concourse.masks import make_identity

F32 = mybir.dt.float32
BF16 = mybir.dt.bfloat16
I32 = mybir.dt.int32
U32 = mybir.dt.uint32
U8 = mybir.dt.uint8
FP8X4 = mybir.dt.float8_e4m3fn_x4
FP4X4 = mybir.dt.float4_e2m1fn_x4
ACT = mybir.ActivationFunctionType
ALU = mybir.AluOpType

P = 128
BATCH = 1024
HIDDEN = 1024
LATENT = 384
XG = 512
K_PASS = 512
PASSES = (XG + HIDDEN) // K_PASS
WORDS = K_PASS // 2
TILES = BATCH // P
PAIRS = TILES // 2
BANK = 512
HALVES = BATCH // BANK
TILES_PER_HALF = BANK // P
UNITS = HIDDEN // P
GATE_R, GATE_Z, GATE_N = 0, 1, 2

FLOPS = 2 * BATCH * 3 * HIDDEN * (XG + HIDDEN)


def tile_rssm_pb_kernel(
    tc,
    sample,
    prev_action,
    prev_state,
    gru_Wih_words,
    gru_Wih_scales,
    gru_Whh_words,
    gru_Whh_scales,
    gru_bih,
    gru_bhh,
    out,
):
    nc = tc.nc
    with ExitStack() as ctx:
        ctx.enter_context(tc.manual_schedule())
        resident = ctx.enter_context(tc.tile_pool(name="resident", bufs=1))
        work = ctx.enter_context(tc.tile_pool(name="work", bufs=4))
        outgoing = ctx.enter_context(tc.tile_pool(name="outgoing", bufs=16))

        xg_rows = resident.tile([P, TILES, XG], BF16)
        state_rows = resident.tile([P, TILES, HIDDEN], BF16)
        pass_words = [
            xg_rows[:].bitcast(F32),
            state_rows[:].bitcast(F32)[:, :, 0:WORDS],
            state_rows[:].bitcast(F32)[:, :, WORDS : 2 * WORDS],
        ]
        x_codes = resident.tile([P, PASSES, BATCH], U32, align_bytes=64)
        x_scales = resident.tile([P, PASSES, BATCH], U8, align_bytes=64)
        w_codes = [
            resident.tile([P, PASSES, 2 * HIDDEN], U8, align_bytes=64, name="w_codes_%d" % gate) for gate in range(3)
        ]
        w_scales = [
            resident.tile([P, PASSES, HIDDEN], U8, align_bytes=64, name="w_scales_%d" % gate) for gate in range(3)
        ]
        z_pre = resident.tile([P, TILES, HIDDEN], F32)
        carried = resident.tile([P, TILES, HIDDEN], F32)
        identity = resident.tile([P, P], F32)
        bias_rows = resident.tile([P, P], BF16)
        bias_rows_f32 = resident.tile([P, P], F32)
        z_rows = resident.tile([P, UNITS], BF16)
        bias_z = resident.tile([P, HIDDEN], F32)
        bias_cols = resident.tile([P, P], F32)
        bias_r = resident.tile([P, UNITS], F32)

        nc.vector.memset(bias_rows[:].bitcast(I32), 0)
        nc.vector.memset(w_scales[GATE_Z][:].bitcast(I32), 0)
        nc.vector.memset(w_scales[GATE_R][:].bitcast(I32), 0)
        nc.vector.memset(w_scales[GATE_N][:].bitcast(I32), 0)
        make_identity(nc, identity[:])
        z_bih, z_bhh = UNITS * GATE_Z, 32 + UNITS * GATE_Z
        nc.vector.tensor_tensor(
            out=z_rows[:], in0=identity[:, z_bih : z_bih + UNITS], in1=identity[:, z_bhh : z_bhh + UNITS], op=ALU.add
        )
        table_probe = resident.tile([P, 1], F32)
        nc.scalar.activation(out=table_probe[:], in_=bias_rows[:, 0:1], func=ACT.Sigmoid)

        sample_dram = sample.rearrange("(p i) c -> p i c", i=TILES)
        action_dram = prev_action.rearrange("(p i) c -> p i c", i=TILES)
        state_dram = prev_state.rearrange("(p i) c -> p i c", i=TILES)
        out_rows = out.rearrange("(p i) h -> p i h", i=TILES)

        def load_xg(pair):
            tiles = slice(2 * pair, 2 * pair + 2)
            nc.sync.dma_start(out=xg_rows[:, tiles, 0:LATENT], in_=sample_dram[:, tiles, :])
            nc.sync.dma_start(out=xg_rows[:, tiles, LATENT:XG], in_=action_dram[:, tiles, :])

        def load_state(pair):
            tiles = slice(2 * pair, 2 * pair + 2)
            nc.sync.dma_start(out=state_rows[:, tiles, :], in_=state_dram[:, tiles, :])

        def load_input_codes(gate):
            cols = slice(2 * HIDDEN * gate, 2 * HIDDEN * (gate + 1))
            nc.sync.dma_start(out=w_codes[gate][:, 0, :].bitcast(I32), in_=gru_Wih_words[0, :, cols].bitcast(I32))

        def load_state_codes(gate):
            cols = slice(2 * HIDDEN * gate, 2 * HIDDEN * (gate + 1))
            nc.sync.dma_start(
                out=w_codes[gate][:, 1:PASSES, :].bitcast(I32),
                in_=gru_Whh_words[:, :, cols].rearrange("g p c -> p g c").bitcast(I32),
            )

        def load_input_scales(gate):
            cols = slice(HIDDEN * gate, HIDDEN * (gate + 1))
            for s in range(4):
                nc.sync.dma_start(
                    out=w_scales[gate][s:P:32, 0, :].bitcast(I32), in_=gru_Wih_scales[0, s:16:4, cols].bitcast(I32)
                )

        def load_state_scales(gate):
            cols = slice(HIDDEN * gate, HIDDEN * (gate + 1))
            for s in range(4):
                nc.sync.dma_start(
                    out=w_scales[gate][s:P:32, 1:PASSES, :].bitcast(I32),
                    in_=gru_Whh_scales[:, s:16:4, cols].rearrange("g q n -> q g n").bitcast(I32),
                )

        nc.gpsimd.dma_start(out=bias_rows[0 : 3 * UNITS, :], in_=gru_bih.rearrange("(r c) -> r c", c=P))
        nc.gpsimd.dma_start(out=bias_rows[32 : 32 + 3 * UNITS, :], in_=gru_bhh.rearrange("(r c) -> r c", c=P))
        for pair in range(PAIRS):
            load_xg(pair)
            if pair == PAIRS - 1:
                load_input_scales(GATE_Z)
            load_state(pair)
        load_state_scales(GATE_Z)
        load_input_codes(GATE_Z)
        load_state_codes(GATE_Z)
        for gate in (GATE_R, GATE_N):
            load_input_scales(gate)
            load_input_codes(gate)
            load_state_scales(gate)
            load_state_codes(gate)

        with tc.psum_pool(name="psum_update", bufs=4, reuse_waits="tile") as psum:

            def flip(pair, g, copier):
                flipped = psum.tile([P, 2, 2, P], F32, tag="flipped")
                for h in range(2):
                    for u in range(2):
                        nc.tensor.transpose(
                            flipped[:, h, u, :],
                            pass_words[g][:, 2 * pair + h, u:WORDS:2],
                            identity[:],
                        )
                grouped = work.tile([P, 2 * K_PASS], BF16, align_bytes=64)
                copier(
                    out=grouped[:].bitcast(F32).rearrange("p (h b u) -> p h b u", h=2, u=2),
                    in_=flipped[:].rearrange("p h u b -> p h b u"),
                )
                return grouped

            def quantise(pair, g, grouped):
                cols = slice(2 * P * pair, 2 * P * (pair + 1))
                nc.vector.quantize_mx(
                    out=x_codes[:, g, cols].bitcast(FP8X4), scales=x_scales[:, g, cols], in_=grouped[:]
                )

            def quantise_pair(pair):
                grouped_tiles = []
                for g in range(PASSES):
                    even = (PASSES * pair + g) % 2 == 0
                    grouped_tiles.append(flip(pair, g, nc.vector.tensor_copy if even else nc.scalar.copy))
                for g in range(PASSES):
                    quantise(pair, g, grouped_tiles[g])

            def repeat_z_biases():
                for half in range(HALVES):
                    repeated = psum.tile([P, TILES_PER_HALF, P], F32, tag="update")
                    for c in range(TILES_PER_HALF):
                        j = TILES_PER_HALF * half + c
                        nc.tensor.matmul(
                            repeated[:, c, :],
                            lhsT=z_rows[:, j : j + 1].to_broadcast([P, P]),
                            rhs=bias_rows[:],
                            start=True,
                            stop=True,
                        )
                    nc.scalar.copy(
                        out=bias_z[:, BANK * half : BANK * (half + 1)], in_=repeated[:].rearrange("p c n -> p (c n)")
                    )

            def turn_biases():
                turned = psum.tile([P, P], F32, tag="flipped")
                nc.tensor.transpose(turned[:], bias_rows_f32[:], identity[:])
                nc.scalar.copy(out=bias_cols[:], in_=turned[:])

            def add_reset_biases():
                r_bih, r_bhh = UNITS * GATE_R, 32 + UNITS * GATE_R
                nc.vector.tensor_tensor(
                    out=bias_r[:], in0=bias_cols[:, r_bih : r_bih + UNITS], in1=bias_cols[:, r_bhh : r_bhh + UNITS], op=ALU.add
                )

            def open_update():
                return [psum.tile([P, BANK], F32, tag="update", name="update") for half in range(HALVES)]

            def update_passes(i, banks, g):
                rows = slice(P * i, P * (i + 1))
                for half in range(HALVES):
                    nc.tensor.matmul_mx(
                        out=banks[half][:],
                        lhsT=x_codes[:, g, rows].bitcast(FP8X4),
                        lhsT_scale=x_scales[:, g, rows],
                        rhs=w_codes[GATE_Z][:, g, 2 * BANK * half : 2 * BANK * (half + 1)].bitcast(FP4X4),
                        rhs_scale=w_scales[GATE_Z][:, g, BANK * half : BANK * (half + 1)],
                        start=(g == 0),
                        stop=(g == PASSES - 1),
                    )

            def finish_update(i, banks):
                for half in range(HALVES):
                    cols = slice(BANK * half, BANK * (half + 1))
                    nc.vector.tensor_tensor(out=z_pre[:, i, cols], in0=banks[half][:], in1=bias_z[:, cols], op=ALU.add)
                    nc.scalar.activation(out=carried[:, i, cols], in_=z_pre[:, i, cols], func=ACT.Sigmoid)
                    nc.gpsimd.tensor_tensor(
                        out=carried[:, i, cols],
                        in0=carried[:, i, cols],
                        in1=state_rows[:, i, cols],
                        op=ALU.mult,
                    )

            def update_gate(i):
                banks = open_update()
                for g in range(PASSES):
                    update_passes(i, banks, g)
                finish_update(i, banks)

            for pair in range(PAIRS - 1):
                quantise_pair(pair)
            nc.vector.tensor_copy(out=bias_rows_f32[:], in_=bias_rows[:])
            quantise_pair(PAIRS - 1)
            repeat_z_biases()
            turn_biases()
            update_gate(0)
            update_gate(1)
            add_reset_biases()
            for i in range(2, TILES):
                update_gate(i)

        with tc.psum_pool(name="psum_candidate", bufs=2, reuse_waits="tile") as psum:

            def weights_stationary(acc, gate, j, g, half, start, stop):
                cols = slice(BANK * half, BANK * (half + 1))
                nc.tensor.matmul_mx(
                    out=acc[:],
                    lhsT=w_codes[gate][:, g, 2 * P * j : 2 * P * (j + 1)].bitcast(FP4X4),
                    lhsT_scale=w_scales[gate][:, g, P * j : P * (j + 1)],
                    rhs=x_codes[:, g, cols].bitcast(FP8X4),
                    rhs_scale=x_scales[:, g, cols],
                    start=start,
                    stop=stop,
                )

            def reset_passes(j, half):
                reset_sum = psum.tile([P, BANK], F32)
                for g in range(PASSES):
                    weights_stationary(reset_sum, GATE_R, j, g, half, start=(g == 0), stop=(g == PASSES - 1))
                return reset_sum

            def state_passes(j, half):
                state_sum = psum.tile([P, BANK], F32)
                for g in range(1, PASSES):
                    weights_stationary(state_sum, GATE_N, j, g, half, start=(g == 1), stop=(g == PASSES - 1))
                return state_sum

            def input_pass(j, half):
                input_sum = psum.tile([P, BANK], F32)
                weights_stationary(input_sum, GATE_N, j, 0, half, start=True, stop=True)
                return input_sum

            def reset_gate(j, reset_sum):
                reset = work.tile([P, BANK], F32)
                nc.scalar.activation(out=reset[:], in_=reset_sum[:], func=ACT.Sigmoid, bias=bias_r[:, j : j + 1])
                return reset

            def gate_state(j, state_sum, reset):
                n_bhh = 32 + UNITS * GATE_N + j
                gated = work.tile([P, BANK], F32)
                nc.vector.scalar_tensor_tensor(
                    out=gated[:],
                    in0=state_sum[:],
                    scalar=bias_cols[:, n_bhh : n_bhh + 1],
                    in1=reset[:],
                    op0=ALU.add,
                    op1=ALU.mult,
                )
                return gated

            def add_input(gated, input_sum, cols):
                nc.vector.tensor_tensor(out=gated[:, cols], in0=gated[:, cols], in1=input_sum[:, cols], op=ALU.add)

            def fresh_share(j):
                fresh = work.tile([P, TILES, P], F32)
                nc.scalar.activation(out=fresh[:], in_=z_pre[:, :, P * j : P * (j + 1)], func=ACT.Sigmoid, scale=-1.0)
                return fresh

            def candidate_values(j, gated, new, cols):
                n_bih = UNITS * GATE_N + j
                nc.scalar.activation(
                    out=new[:, cols], in_=gated[:, cols], func=ACT.Tanh, bias=bias_cols[:, n_bih : n_bih + 1]
                )

            def candidate(j):
                reset_sums = [reset_passes(j, half) for half in range(HALVES)]
                state_sums = [state_passes(j, half) for half in range(HALVES)]
                input_sums = [input_pass(j, half) for half in range(HALVES)]
                inner = []
                for half in range(HALVES):
                    inner.append(gate_state(j, state_sums[half], reset_gate(j, reset_sums[half])))
                for half in range(HALVES):
                    add_input(inner[half], input_sums[half], slice(0, BANK))
                fresh = fresh_share(j)
                news = []
                for half in range(HALVES):
                    new = work.tile([P, BANK], F32)
                    candidate_values(j, inner[half], new, slice(0, BANK))
                    news.append(new)
                return news, fresh

            def turn(turned, new, first, count):
                for c in range(count):
                    nc.tensor.transpose(turned[:, c, :], new[:, P * (first + c) : P * (first + c + 1)], identity[:])

            def scale_new(turned, fresh, tiles):
                belief = outgoing.tile([P, TILES_PER_HALF, P], F32)
                count = tiles.stop - tiles.start
                nc.vector.tensor_tensor(
                    out=belief[:, 0:count, :], in0=turned[:, 0:count, :], in1=fresh[:, tiles, :], op=ALU.mult
                )
                return belief

            def add_and_store(j, belief, tiles, adder):
                cols = slice(P * j, P * (j + 1))
                count = tiles.stop - tiles.start
                adder.tensor_tensor(
                    out=belief[:, 0:count, :], in0=belief[:, 0:count, :], in1=carried[:, tiles, cols], op=ALU.add
                )
                nc.sync.dma_start(out=out_rows[:, tiles, cols], in_=belief[:, 0:count, :])

            def half_tiles(half):
                return slice(TILES_PER_HALF * half, TILES_PER_HALF * (half + 1))

            def turn_unit(news):
                turned_halves = []
                for half in range(HALVES):
                    turned = psum.tile([P, TILES_PER_HALF, P], F32)
                    turn(turned, news[half], 0, TILES_PER_HALF)
                    turned_halves.append(turned)
                return turned_halves

            def blend_and_store(j, news, fresh):
                turned_halves = turn_unit(news)
                beliefs = [scale_new(turned_halves[half], fresh, half_tiles(half)) for half in range(HALVES)]
                for half in range(HALVES):
                    add_and_store(j, beliefs[half], half_tiles(half), nc.gpsimd)

            waiting = candidate(0)
            for j in range(1, UNITS - 1):
                following = candidate(j)
                blend_and_store(j - 1, waiting[0], waiting[1])
                waiting = following

            last = UNITS - 1
            news, fresh = waiting
            last_news, last_fresh = candidate(last)
            turned_halves = turn_unit(news)
            last_turned = [
                psum.tile([P, TILES_PER_HALF, P], F32, tag="reset_sum", name="turned"),
                psum.tile([P, TILES_PER_HALF, P], F32, tag="reset_sum", name="turned"),
            ]
            for half in range(HALVES):
                turn(last_turned[half], last_news[half], 0, TILES_PER_HALF)
            beliefs = [scale_new(turned_halves[half], fresh, half_tiles(half)) for half in range(HALVES)]
            add_and_store(last - 1, beliefs[0], half_tiles(0), nc.gpsimd)
            last_beliefs = [scale_new(last_turned[half], last_fresh, half_tiles(half)) for half in range(HALVES)]
            add_and_store(last - 1, beliefs[1], half_tiles(1), nc.vector)
            for half in range(HALVES):
                add_and_store(last, last_beliefs[half], half_tiles(half), nc.vector)
